import numpy as np
import ml_dtypes

BF16 = ml_dtypes.bfloat16


def bf(x):
    return np.asarray(x, np.float32).astype(BF16)


def f32(x):
    return np.asarray(x, np.float32)


def f64(x):
    return np.asarray(x).astype(np.float64)


def striped(idx):
    return np.tile(idx.reshape(-1, 16).T, (8, 1))


C, F, M, S, H, K, N = 512, 128, 512, 256, 128, 6, 768


def setup_inputs():
    return {"x": f32(np.random.standard_normal((C, S))), "fatoms": bf(np.random.standard_normal((F, H))), "w_f": bf(np.random.standard_normal((F, M)) / np.sqrt(F)), "w_h": bf(0.5 * np.random.standard_normal((C, M)) / np.sqrt(C)), "b": f32(0.3 * np.random.standard_normal((M, 1))), "offs": striped(np.concatenate([np.random.permutation(S)[:H] for _ in range(K)]))}


def reference(x, fatoms, w_f, w_h, b, offs):
    idx = offs[:16].T.reshape(-1)
    msg = np.maximum(f64(x), 0.0)
    nei = msg[:, idx].reshape(C, K, H).sum(axis=1)
    return np.maximum(f64(w_f).T @ f64(fatoms) + f64(w_h).T @ nei + f64(b), 0.0)

@@ -1,0 +1,89 @@
+import concourse.mybir as mybir
+from concourse.masks import make_identity
+
+F32, BF16, U16 = mybir.dt.float32, mybir.dt.bfloat16, mybir.dt.uint16
+ADD, MAX = mybir.AluOpType.add, mybir.AluOpType.max
+RELU = mybir.ActivationFunctionType.Relu
+
+P = 128
+C, F, M = 512, 128, 512
+S, H, K = 256, 128, 6
+N = K * H
+CB, MB = C // P, M // P
+PAIR = 2 * H
+COLS = PAIR // 16
+
+FLOPS = 2 * M * H * (F + C)
+
+
+def tile_mpn_kernel(tc, x, fatoms, w_f, w_h, b, offs, out):
+    nc = tc.nc
+    with (
+        tc.tile_pool(name="held", bufs=1) as held,
+        tc.psum_pool(name="psum", bufs=1) as psum,
+    ):
+        raw = [held.tile([P, S], F32, name=f"raw{c}", tag=f"raw{c}") for c in range(CB)]
+        for h in range(2):
+            nc.sync.dma_start(raw[0][:, h * H : (h + 1) * H], x[0:P, h * H : (h + 1) * H])
+        offsets = held.tile([P, N // 16], U16, name="offsets")
+        nc.sync.dma_start(offsets[:], offs)
+        for c in range(1, CB):
+            nc.sync.dma_start(raw[c][:], x[c * P : (c + 1) * P, :])
+        atoms = held.tile([P, H], BF16, name="atoms")
+        nc.sync.dma_start(atoms[:], fatoms)
+        wf = held.tile([P, M], BF16, name="wf")
+        nc.sync.dma_start(wf[:], w_f)
+        wh = held.tile([P, CB, M], BF16, name="wh")
+        for c in range(2):
+            nc.sync.dma_start(wh[:, c, :], w_h[c * P : (c + 1) * P, :])
+        nc.sync.dma_start(wh[:, 2:CB, :], w_h[2 * P : CB * P, :].rearrange("(c p) m -> p c m", p=P))
+        bias = held.tile([P, MB], F32, name="bias")
+        with nc.allow_non_contiguous_dma(reason="512 biases, one to a partition"):
+            nc.sync.dma_start(bias[:], b.rearrange("(t p) o -> p (t o)", p=P))
+        zeros = held.tile([P, PAIR], F32, name="zeros")
+        nc.vector.memset(zeros[:], 0.0)
+        ident = held.tile([P, P], F32, name="ident")
+        make_identity(nc, ident[:])
+
+        msg = [held.tile([P, S], F32, name=f"msg{c}") for c in range(CB)]
+        for h in range(2):
+            nc.vector.tensor_scalar_max(msg[0][:, h * H : (h + 1) * H], raw[0][:, h * H : (h + 1) * H], 0.0)
+        for c in range(1, CB):
+            nc.scalar.activation(msg[c][:], raw[c][:], RELU)
+
+        acc = [psum.tile([P, H], F32, name=f"acc{t}") for t in range(MB)]
+        for t in range(MB):
+            nc.tensor.matmul(acc[t][:], wf[:, t * P : (t + 1) * P], atoms[:], start=True, stop=False)
+
+        for first in range(0, CB, 2):
+            both = (first, first + 1)
+            halves = {c: zeros for c in both}
+            for j in range(K // 2):
+                for c in both:
+                    picked = msg[c][:].indirect(offsets[:, j * COLS : (j + 1) * COLS])
+                    place = "raw1" if (c, j) == (0, 1) else f"sum{c}_{j}"
+                    longer = held.tile([P, PAIR], F32, name=f"sum{c}_{j}", tag=place)
+                    nc.vector.tensor_tensor(longer[:], picked, halves[c][:], ADD)
+                    halves[c] = longer
+            for c in both:
+                nei_bf = held.tile([P, H], BF16, name=f"nei_bf{c}")
+                if first == 0:
+                    joined = psum.tile([P, H], F32, name=f"joined{c}")
+                    nc.tensor.matmul(joined[:], ident[:], halves[c][:, :H], start=True, stop=False)
+                    nc.tensor.matmul(joined[:], ident[:], halves[c][:, H:], start=False, stop=True)
+                    nc.scalar.copy(nei_bf[:], joined[:])
+                else:
+                    nc.vector.tensor_tensor(nei_bf[:], halves[c][:, :H], halves[c][:, H:], ADD)
+                for t in range(MB):
+                    nc.tensor.matmul(
+                        acc[t][:], wh[:, c, t * P : (t + 1) * P], nei_bf[:], start=False, stop=(c == CB - 1)
+                    )
+
+        for t in range(MB):
+            res = held.tile([P, H], F32, name=f"res{t}")
+            if t % 2 == 1:
+                nc.scalar.activation(res[:], acc[t][:], RELU, bias=bias[:, t : t + 1])
+                nc.scalar.dma_start(out[t * P : (t + 1) * P, :], res[:])
+            else:
+                nc.vector.tensor_scalar(res[:], acc[t][:], bias[:, t : t + 1], 0.0, op0=ADD, op1=MAX)
+                nc.sync.dma_start(out[t * P : (t + 1) * P, :], res[:])

@@ -23,8 +23,7 @@ def tile_mpn_kernel(tc, x, fatoms, w_f, w_h, b, offs, out):
         tc.psum_pool(name="psum", bufs=1) as psum,
     ):
         raw = [held.tile([P, S], F32, name=f"raw{c}", tag=f"raw{c}") for c in range(CB)]
-        for h in range(2):
-            nc.sync.dma_start(raw[0][:, h * H : (h + 1) * H], x[0:P, h * H : (h + 1) * H])
+        nc.sync.dma_start(raw[0][:], x[0:P, :])
         offsets = held.tile([P, N // 16], U16, name="offsets")
         nc.sync.dma_start(offsets[:], offs)
         for c in range(1, CB):
@@ -34,9 +33,8 @@ def tile_mpn_kernel(tc, x, fatoms, w_f, w_h, b, offs, out):
         wf = held.tile([P, M], BF16, name="wf")
         nc.sync.dma_start(wf[:], w_f)
         wh = held.tile([P, CB, M], BF16, name="wh")
-        for c in range(2):
+        for c in range(CB):
             nc.sync.dma_start(wh[:, c, :], w_h[c * P : (c + 1) * P, :])
-        nc.sync.dma_start(wh[:, 2:CB, :], w_h[2 * P : CB * P, :].rearrange("(c p) m -> p c m", p=P))
         bias = held.tile([P, MB], F32, name="bias")
         with nc.allow_non_contiguous_dma(reason="512 biases, one to a partition"):
             nc.sync.dma_start(bias[:], b.rearrange("(t p) o -> p (t o)", p=P))
@@ -46,8 +44,7 @@ def tile_mpn_kernel(tc, x, fatoms, w_f, w_h, b, offs, out):
         make_identity(nc, ident[:])
 
         msg = [held.tile([P, S], F32, name=f"msg{c}") for c in range(CB)]
-        for h in range(2):
-            nc.vector.tensor_scalar_max(msg[0][:, h * H : (h + 1) * H], raw[0][:, h * H : (h + 1) * H], 0.0)
+        nc.vector.tensor_scalar_max(msg[0][:], raw[0][:], 0.0)
         for c in range(1, CB):
             nc.scalar.activation(msg[c][:], raw[c][:], RELU)
 

import concourse.mybir as mybir
from concourse.masks import make_identity

F32, BF16, U16 = mybir.dt.float32, mybir.dt.bfloat16, mybir.dt.uint16
ADD, MAX = mybir.AluOpType.add, mybir.AluOpType.max
RELU = mybir.ActivationFunctionType.Relu

P = 128
C, F, M = 512, 128, 512
S, H, K = 256, 128, 6
N = K * H
CB, MB = C // P, M // P
PAIR = 2 * H
COLS = PAIR // 16

FLOPS = 2 * M * H * (F + C)


def tile_mpn_kernel(tc, x, fatoms, w_f, w_h, b, offs, out):
    nc = tc.nc
    with (
        tc.tile_pool(name="held", bufs=1) as held,
        tc.psum_pool(name="psum", bufs=1) as psum,
    ):
        raw = [held.tile([P, S], F32, name=f"raw{c}", tag=f"raw{c}") for c in range(CB)]
        nc.sync.dma_start(raw[0][:], x[0:P, :])
        offsets = held.tile([P, N // 16], U16, name="offsets")
        nc.sync.dma_start(offsets[:], offs)
        for c in range(1, CB):
            nc.sync.dma_start(raw[c][:], x[c * P : (c + 1) * P, :])
        atoms = held.tile([P, H], BF16, name="atoms")
        nc.sync.dma_start(atoms[:], fatoms)
        wf = held.tile([P, M], BF16, name="wf")
        nc.sync.dma_start(wf[:], w_f)
        wh = held.tile([P, CB, M], BF16, name="wh")
        for c in range(CB):
            nc.sync.dma_start(wh[:, c, :], w_h[c * P : (c + 1) * P, :])
        bias = held.tile([P, MB], F32, name="bias")
        with nc.allow_non_contiguous_dma(reason="512 biases, one to a partition"):
            nc.sync.dma_start(bias[:], b.rearrange("(t p) o -> p (t o)", p=P))
        zeros = held.tile([P, PAIR], F32, name="zeros")
        nc.vector.memset(zeros[:], 0.0)
        ident = held.tile([P, P], F32, name="ident")
        make_identity(nc, ident[:])

        msg = [held.tile([P, S], F32, name=f"msg{c}") for c in range(CB)]
        nc.vector.tensor_scalar_max(msg[0][:], raw[0][:], 0.0)
        for c in range(1, CB):
            nc.scalar.activation(msg[c][:], raw[c][:], RELU)

        acc = [psum.tile([P, H], F32, name=f"acc{t}") for t in range(MB)]
        for t in range(MB):
            nc.tensor.matmul(acc[t][:], wf[:, t * P : (t + 1) * P], atoms[:], start=True, stop=False)

        for first in range(0, CB, 2):
            both = (first, first + 1)
            halves = {c: zeros for c in both}
            for j in range(K // 2):
                for c in both:
                    picked = msg[c][:].indirect(offsets[:, j * COLS : (j + 1) * COLS])
                    place = "raw1" if (c, j) == (0, 1) else f"sum{c}_{j}"
                    longer = held.tile([P, PAIR], F32, name=f"sum{c}_{j}", tag=place)
                    nc.vector.tensor_tensor(longer[:], picked, halves[c][:], ADD)
                    halves[c] = longer
            for c in both:
                nei_bf = held.tile([P, H], BF16, name=f"nei_bf{c}")
                if first == 0:
                    joined = psum.tile([P, H], F32, name=f"joined{c}")
                    nc.tensor.matmul(joined[:], ident[:], halves[c][:, :H], start=True, stop=False)
                    nc.tensor.matmul(joined[:], ident[:], halves[c][:, H:], start=False, stop=True)
                    nc.scalar.copy(nei_bf[:], joined[:])
                else:
                    nc.vector.tensor_tensor(nei_bf[:], halves[c][:, :H], halves[c][:, H:], ADD)
                for t in range(MB):
                    nc.tensor.matmul(
                        acc[t][:], wh[:, c, t * P : (t + 1) * P], nei_bf[:], start=False, stop=(c == CB - 1)
                    )

        for t in range(MB):
            res = held.tile([P, H], F32, name=f"res{t}")
            if t % 2 == 1:
                nc.scalar.activation(res[:], acc[t][:], RELU, bias=bias[:, t : t + 1])
                nc.scalar.dma_start(out[t * P : (t + 1) * P, :], res[:])
            else:
                nc.vector.tensor_scalar(res[:], acc[t][:], bias[:, t : t + 1], 0.0, op0=ADD, op1=MAX)
                nc.sync.dma_start(out[t * P : (t + 1) * P, :], res[:])
